import numpy as np
import ml_dtypes

BF16 = ml_dtypes.bfloat16


def bf(x):
    return np.asarray(x, np.float32).astype(BF16)


def f32(x):
    return np.asarray(x, np.float32)


def f64(x):
    return np.asarray(x).astype(np.float64)


def striped(idx):
    return np.tile(idx.reshape(-1, 16).T, (8, 1))


C, S, N, SEG, W, M = 128, 1024, 512, 128, 4, 16
NW = SEG + M


def setup_inputs():
    return {'tok_emb': f32(np.random.standard_normal((C, S))), 'pos_seg': f32(0.5 * np.random.standard_normal((C, NW))), 'pos_win': f32(0.5 * np.random.standard_normal((C, W))), 'mems': f32(np.random.standard_normal((C, M))), 'offs': striped(np.random.permutation(np.tile(np.arange(S), 2))[:N])}


def reference(tok_emb, pos_seg, pos_win, mems, offs):
    idx = offs[:16].T.reshape(-1)
    tok = f64(tok_emb)[:, idx].reshape(C, W, SEG)
    mem = np.broadcast_to(f64(mems)[:, None, :], (C, W, M))
    x = np.concatenate([mem, tok], axis=2)
    x = x + f64(pos_win)[:, :, None] + f64(pos_seg)[:, None, :]
    return x.reshape(C, W * NW)

@@ -1,0 +1,54 @@
+import concourse.mybir as mybir
+
+F32 = mybir.dt.float32
+U16 = mybir.dt.uint16
+ADD = mybir.AluOpType.add
+
+C = 128
+VOCAB = 1024
+N = 512
+WINDOWS = 4
+SEG = 128
+MEM = 16
+PLACES = MEM + SEG
+PER_COLUMN = 16
+
+
+def tile_mactransformer_kernel(tc, tok_emb, pos_seg, pos_win, mems, offs, out):
+    nc = tc.nc
+    with tc.tile_pool(name="held", bufs=1) as held:
+        offsets = held.tile([C, N // PER_COLUMN], U16, name="offsets")
+        table = held.tile([C, VOCAB], F32, name="table")
+        seg = held.tile([C, PLACES], F32, name="seg")
+        win = held.tile([C, WINDOWS], F32, name="win")
+        mem = held.tile([C, MEM], F32, name="mem")
+        pos = held.tile([C, N], F32, name="pos")
+        result = held.tile([C, WINDOWS * PLACES], F32, name="result")
+
+        nc.sync.dma_start(offsets[:], offs)
+        nc.sync.dma_start(table[:], tok_emb)
+        nc.sync.dma_start(seg[:], pos_seg)
+        nc.sync.dma_start(win[:], pos_win)
+        nc.sync.dma_start(mem[:], mems)
+
+        nc.vector.tensor_tensor(mem[:], mem[:], seg[:, 0:MEM], ADD)
+
+        for w in range(WINDOWS):
+            nc.vector.tensor_scalar_add(
+                result[:, w * PLACES : w * PLACES + MEM], mem[:], win[:, w : w + 1]
+            )
+            nc.vector.tensor_scalar_add(
+                pos[:, w * SEG : (w + 1) * SEG], seg[:, MEM:PLACES], win[:, w : w + 1]
+            )
+
+        columns = SEG // PER_COLUMN
+        for w in range(WINDOWS):
+            picked = table[:].indirect(offsets[:, w * columns : (w + 1) * columns])
+            nc.vector.tensor_tensor(
+                result[:, w * PLACES + MEM : (w + 1) * PLACES],
+                picked,
+                pos[:, w * SEG : (w + 1) * SEG],
+                ADD,
+            )
+
+        nc.sync.dma_start(out, result[:])

@@ -27,9 +27,9 @@ def tile_mactransformer_kernel(tc, tok_emb, pos_seg, pos_win, mems, offs, out):
 
         nc.sync.dma_start(offsets[:], offs)
         nc.sync.dma_start(table[:], tok_emb)
-        nc.sync.dma_start(seg[:], pos_seg)
-        nc.sync.dma_start(win[:], pos_win)
-        nc.sync.dma_start(mem[:], mems)
+        nc.scalar.dma_start(seg[:], pos_seg)
+        nc.scalar.dma_start(win[:], pos_win)
+        nc.scalar.dma_start(mem[:], mems)
 
         nc.vector.tensor_tensor(mem[:], mem[:], seg[:, 0:MEM], ADD)
 

@@ -50,5 +50,7 @@ def tile_mactransformer_kernel(tc, tok_emb, pos_seg, pos_win, mems, offs, out):
                 pos[:, w * SEG : (w + 1) * SEG],
                 ADD,
             )
-
-        nc.sync.dma_start(out, result[:])
+            nc.sync.dma_start(
+                out[:, w * PLACES : (w + 1) * PLACES],
+                result[:, w * PLACES : (w + 1) * PLACES],
+            )

@@ -12,18 +12,21 @@ SEG = 128
 MEM = 16
 PLACES = MEM + SEG
 PER_COLUMN = 16
+COLUMNS = SEG // PER_COLUMN
 
 
 def tile_mactransformer_kernel(tc, tok_emb, pos_seg, pos_win, mems, offs, out):
     nc = tc.nc
+    out_windows = out.rearrange("c (w s) -> c w s", w=WINDOWS)
     with tc.tile_pool(name="held", bufs=1) as held:
         offsets = held.tile([C, N // PER_COLUMN], U16, name="offsets")
         table = held.tile([C, VOCAB], F32, name="table")
         seg = held.tile([C, PLACES], F32, name="seg")
         win = held.tile([C, WINDOWS], F32, name="win")
         mem = held.tile([C, MEM], F32, name="mem")
+        memory = held.tile([C, WINDOWS * MEM], F32, name="memory")
         pos = held.tile([C, N], F32, name="pos")
-        result = held.tile([C, WINDOWS * PLACES], F32, name="result")
+        tokens = held.tile([C, N], F32, name="tokens")
 
         nc.sync.dma_start(offsets[:], offs)
         nc.sync.dma_start(table[:], tok_emb)
@@ -32,25 +35,29 @@ def tile_mactransformer_kernel(tc, tok_emb, pos_seg, pos_win, mems, offs, out):
         nc.scalar.dma_start(mem[:], mems)
 
         nc.vector.tensor_tensor(mem[:], mem[:], seg[:, 0:MEM], ADD)
-
         for w in range(WINDOWS):
             nc.vector.tensor_scalar_add(
-                result[:, w * PLACES : w * PLACES + MEM], mem[:], win[:, w : w + 1]
+                memory[:, w * MEM : (w + 1) * MEM], mem[:], win[:, w : w + 1]
             )
+        nc.scalar.dma_start(
+            out_windows[:, :, 0:MEM],
+            memory[:].rearrange("c (w m) -> c w m", w=WINDOWS),
+        )
+
+        for w in range(WINDOWS):
             nc.vector.tensor_scalar_add(
                 pos[:, w * SEG : (w + 1) * SEG], seg[:, MEM:PLACES], win[:, w : w + 1]
             )
 
-        columns = SEG // PER_COLUMN
         for w in range(WINDOWS):
-            picked = table[:].indirect(offsets[:, w * columns : (w + 1) * columns])
+            picked = table[:].indirect(offsets[:, w * COLUMNS : (w + 1) * COLUMNS])
             nc.vector.tensor_tensor(
-                result[:, w * PLACES + MEM : (w + 1) * PLACES],
+                tokens[:, w * SEG : (w + 1) * SEG],
                 picked,
                 pos[:, w * SEG : (w + 1) * SEG],
                 ADD,
             )
             nc.sync.dma_start(
-                out[:, w * PLACES : (w + 1) * PLACES],
-                result[:, w * PLACES : (w + 1) * PLACES],
+                out[:, w * PLACES + MEM : (w + 1) * PLACES],
+                tokens[:, w * SEG : (w + 1) * SEG],
             )

@@ -28,11 +28,11 @@ def tile_mactransformer_kernel(tc, tok_emb, pos_seg, pos_win, mems, offs, out):
         pos = held.tile([C, N], F32, name="pos")
         tokens = held.tile([C, N], F32, name="tokens")
 
-        nc.sync.dma_start(offsets[:], offs)
-        nc.sync.dma_start(table[:], tok_emb)
-        nc.scalar.dma_start(seg[:], pos_seg)
+        nc.sync.dma_start(seg[:], pos_seg)
         nc.scalar.dma_start(win[:], pos_win)
         nc.scalar.dma_start(mem[:], mems)
+        nc.sync.dma_start(offsets[:], offs)
+        nc.sync.dma_start(table[:], tok_emb)
 
         nc.vector.tensor_tensor(mem[:], mem[:], seg[:, 0:MEM], ADD)
         for w in range(WINDOWS):

@@ -49,15 +49,17 @@ def tile_mactransformer_kernel(tc, tok_emb, pos_seg, pos_win, mems, offs, out):
                 pos[:, w * SEG : (w + 1) * SEG], seg[:, MEM:PLACES], win[:, w : w + 1]
             )
 
-        for w in range(WINDOWS):
-            picked = table[:].indirect(offsets[:, w * COLUMNS : (w + 1) * COLUMNS])
+        for first, last in ((0, 3), (3, 4)):
+            picked = table[:].indirect(offsets[:, first * COLUMNS : last * COLUMNS])
             nc.vector.tensor_tensor(
-                tokens[:, w * SEG : (w + 1) * SEG],
+                tokens[:, first * SEG : last * SEG],
                 picked,
-                pos[:, w * SEG : (w + 1) * SEG],
+                pos[:, first * SEG : last * SEG],
                 ADD,
             )
             nc.sync.dma_start(
-                out[:, w * PLACES + MEM : (w + 1) * PLACES],
-                tokens[:, w * SEG : (w + 1) * SEG],
+                out_windows[:, first:last, MEM:PLACES],
+                tokens[:, first * SEG : last * SEG].rearrange(
+                    "c (w s) -> c w s", s=SEG
+                ),
             )

@@ -49,7 +49,7 @@ def tile_mactransformer_kernel(tc, tok_emb, pos_seg, pos_win, mems, offs, out):
                 pos[:, w * SEG : (w + 1) * SEG], seg[:, MEM:PLACES], win[:, w : w + 1]
             )
 
-        for first, last in ((0, 3), (3, 4)):
+        for first, last, queue in ((0, 3, nc.scalar), (3, 4, nc.sync)):
             picked = table[:].indirect(offsets[:, first * COLUMNS : last * COLUMNS])
             nc.vector.tensor_tensor(
                 tokens[:, first * SEG : last * SEG],
@@ -57,7 +57,7 @@ def tile_mactransformer_kernel(tc, tok_emb, pos_seg, pos_win, mems, offs, out):
                 pos[:, first * SEG : last * SEG],
                 ADD,
             )
-            nc.sync.dma_start(
+            queue.dma_start(
                 out_windows[:, first:last, MEM:PLACES],
                 tokens[:, first * SEG : last * SEG].rearrange(
                     "c (w s) -> c w s", s=SEG

@@ -49,7 +49,7 @@ def tile_mactransformer_kernel(tc, tok_emb, pos_seg, pos_win, mems, offs, out):
                 pos[:, w * SEG : (w + 1) * SEG], seg[:, MEM:PLACES], win[:, w : w + 1]
             )
 
-        for first, last, queue in ((0, 3, nc.scalar), (3, 4, nc.sync)):
+        for first, last, queue in ((0, 2, nc.scalar), (2, 4, nc.sync)):
             picked = table[:].indirect(offsets[:, first * COLUMNS : last * COLUMNS])
             nc.vector.tensor_tensor(
                 tokens[:, first * SEG : last * SEG],

@@ -13,6 +13,7 @@ MEM = 16
 PLACES = MEM + SEG
 PER_COLUMN = 16
 COLUMNS = SEG // PER_COLUMN
+PAIR = 2 * PLACES
 
 
 def tile_mactransformer_kernel(tc, tok_emb, pos_seg, pos_win, mems, offs, out):
@@ -24,9 +25,10 @@ def tile_mactransformer_kernel(tc, tok_emb, pos_seg, pos_win, mems, offs, out):
         seg = held.tile([C, PLACES], F32, name="seg")
         win = held.tile([C, WINDOWS], F32, name="win")
         mem = held.tile([C, MEM], F32, name="mem")
-        memory = held.tile([C, WINDOWS * MEM], F32, name="memory")
         pos = held.tile([C, N], F32, name="pos")
-        tokens = held.tile([C, N], F32, name="tokens")
+        odd_memory = held.tile([C, 2 * MEM], F32, name="odd_memory")
+        first_pair = held.tile([C, PAIR], F32, name="first_pair")
+        last_pair = held.tile([C, 2 * SEG], F32, name="last_pair")
 
         nc.sync.dma_start(seg[:], pos_seg)
         nc.scalar.dma_start(win[:], pos_win)
@@ -34,32 +36,42 @@ def tile_mactransformer_kernel(tc, tok_emb, pos_seg, pos_win, mems, offs, out):
         nc.sync.dma_start(offsets[:], offs)
         nc.sync.dma_start(table[:], tok_emb)
 
-        nc.vector.tensor_tensor(mem[:], mem[:], seg[:, 0:MEM], ADD)
-        for w in range(WINDOWS):
-            nc.vector.tensor_scalar_add(
-                memory[:, w * MEM : (w + 1) * MEM], mem[:], win[:, w : w + 1]
-            )
-        nc.scalar.dma_start(
-            out_windows[:, :, 0:MEM],
-            memory[:].rearrange("c (w m) -> c w m", w=WINDOWS),
-        )
-
         for w in range(WINDOWS):
             nc.vector.tensor_scalar_add(
                 pos[:, w * SEG : (w + 1) * SEG], seg[:, MEM:PLACES], win[:, w : w + 1]
             )
 
-        for first, last, queue in ((0, 2, nc.scalar), (2, 4, nc.sync)):
-            picked = table[:].indirect(offsets[:, first * COLUMNS : last * COLUMNS])
-            nc.vector.tensor_tensor(
-                tokens[:, first * SEG : last * SEG],
-                picked,
-                pos[:, first * SEG : last * SEG],
-                ADD,
-            )
-            queue.dma_start(
-                out_windows[:, first:last, MEM:PLACES],
-                tokens[:, first * SEG : last * SEG].rearrange(
-                    "c (w s) -> c w s", s=SEG
-                ),
-            )
+        memory_places = (
+            first_pair[:, 0:MEM],
+            odd_memory[:, 0:MEM],
+            first_pair[:, PAIR - MEM : PAIR],
+            odd_memory[:, MEM : 2 * MEM],
+        )
+        nc.vector.tensor_tensor(mem[:], mem[:], seg[:, 0:MEM], ADD)
+        for w in range(WINDOWS):
+            nc.vector.tensor_scalar_add(memory_places[w], mem[:], win[:, w : w + 1])
+        nc.scalar.dma_start(
+            out.rearrange("c (p s) -> c p s", s=PAIR)[:, :, PLACES : PLACES + MEM],
+            odd_memory[:].rearrange("c (p m) -> c p m", p=2),
+        )
+
+        nc.vector.tensor_tensor(
+            first_pair[:, MEM : PAIR - MEM],
+            table[:].indirect(offsets[:, 0 : 2 * COLUMNS]),
+            pos[:, 0 : 2 * SEG],
+            ADD,
+        )
+        nc.scalar.dma_start(
+            out[:, 0 : 2 * (PLACES + MEM)].rearrange("c (r s) -> c r s", r=2)[:, :, 0:PLACES],
+            first_pair[:].rearrange("c (r s) -> c r s", r=2),
+        )
+        nc.vector.tensor_tensor(
+            last_pair[:],
+            table[:].indirect(offsets[:, 2 * COLUMNS : 4 * COLUMNS]),
+            pos[:, 2 * SEG : 4 * SEG],
+            ADD,
+        )
+        nc.sync.dma_start(
+            out_windows[:, 2:4, MEM:PLACES],
+            last_pair[:].rearrange("c (w s) -> c w s", s=SEG),
+        )

import concourse.mybir as mybir

F32 = mybir.dt.float32
U16 = mybir.dt.uint16
ADD = mybir.AluOpType.add

C = 128
VOCAB = 1024
N = 512
WINDOWS = 4
SEG = 128
MEM = 16
PLACES = MEM + SEG
PER_COLUMN = 16
COLUMNS = SEG // PER_COLUMN
PAIR = 2 * PLACES


def tile_mactransformer_kernel(tc, tok_emb, pos_seg, pos_win, mems, offs, out):
    nc = tc.nc
    out_windows = out.rearrange("c (w s) -> c w s", w=WINDOWS)
    with tc.tile_pool(name="held", bufs=1) as held:
        offsets = held.tile([C, N // PER_COLUMN], U16, name="offsets")
        table = held.tile([C, VOCAB], F32, name="table")
        seg = held.tile([C, PLACES], F32, name="seg")
        win = held.tile([C, WINDOWS], F32, name="win")
        mem = held.tile([C, MEM], F32, name="mem")
        pos = held.tile([C, N], F32, name="pos")
        odd_memory = held.tile([C, 2 * MEM], F32, name="odd_memory")
        first_pair = held.tile([C, PAIR], F32, name="first_pair")
        last_pair = held.tile([C, 2 * SEG], F32, name="last_pair")

        nc.sync.dma_start(seg[:], pos_seg)
        nc.scalar.dma_start(win[:], pos_win)
        nc.scalar.dma_start(mem[:], mems)
        nc.sync.dma_start(offsets[:], offs)
        nc.sync.dma_start(table[:], tok_emb)

        for w in range(WINDOWS):
            nc.vector.tensor_scalar_add(
                pos[:, w * SEG : (w + 1) * SEG], seg[:, MEM:PLACES], win[:, w : w + 1]
            )

        memory_places = (
            first_pair[:, 0:MEM],
            odd_memory[:, 0:MEM],
            first_pair[:, PAIR - MEM : PAIR],
            odd_memory[:, MEM : 2 * MEM],
        )
        nc.vector.tensor_tensor(mem[:], mem[:], seg[:, 0:MEM], ADD)
        for w in range(WINDOWS):
            nc.vector.tensor_scalar_add(memory_places[w], mem[:], win[:, w : w + 1])
        nc.scalar.dma_start(
            out.rearrange("c (p s) -> c p s", s=PAIR)[:, :, PLACES : PLACES + MEM],
            odd_memory[:].rearrange("c (p m) -> c p m", p=2),
        )

        nc.vector.tensor_tensor(
            first_pair[:, MEM : PAIR - MEM],
            table[:].indirect(offsets[:, 0 : 2 * COLUMNS]),
            pos[:, 0 : 2 * SEG],
            ADD,
        )
        nc.scalar.dma_start(
            out[:, 0 : 2 * (PLACES + MEM)].rearrange("c (r s) -> c r s", r=2)[:, :, 0:PLACES],
            first_pair[:].rearrange("c (r s) -> c r s", r=2),
        )
        nc.vector.tensor_tensor(
            last_pair[:],
            table[:].indirect(offsets[:, 2 * COLUMNS : 4 * COLUMNS]),
            pos[:, 2 * SEG : 4 * SEG],
            ADD,
        )
        nc.sync.dma_start(
            out_windows[:, 2:4, MEM:PLACES],
            last_pair[:].rearrange("c (w s) -> c w s", s=SEG),
        )
